import numpy as np
import ml_dtypes


def mxq(x, axis, fmt="e4m3"):
    dtype, down = {"e4m3": (ml_dtypes.float8_e4m3fn, 7), "e5m2": (ml_dtypes.float8_e5m2, 14)}[fmt]
    v = np.moveaxis(np.asarray(x, np.float32).astype(ml_dtypes.bfloat16).astype(np.float64), axis, -1)
    blocks = v.reshape(v.shape[:-1] + (-1, 32))
    amax = np.abs(blocks).max(-1, keepdims=True)
    byte = np.maximum(np.where(amax > 0, np.frexp(amax)[1] - 1 + 127, 0) - down, 1)
    scale = np.exp2(byte - 127.0)
    codes = (blocks / scale).astype(np.float32).astype(dtype).astype(np.float64)
    return np.moveaxis((codes * scale).reshape(v.shape), -1, axis)


WIDE = False


def mx_kscale(k):
    if not WIDE:
        return np.ones(k)
    levels = np.array([10, -10, 5, -5, 0])
    if k % 512:
        return np.exp2(np.random.permutation(np.resize(levels, k // 32))).repeat(32)
    a = np.empty((k // 512, 16))
    for p in range(k // 512):
        a[p, :8] = np.random.permutation(np.resize(levels, 8))
        for g in range(8):
            far = levels[np.abs(levels - a[p, g]) >= 10]
            a[p, g + 8] = far[np.random.randint(len(far))]
    return np.exp2(a.ravel()).repeat(32)


BF16 = ml_dtypes.bfloat16


def bf(x):
    return np.asarray(x, np.float32).astype(BF16)


def f64(x):
    return np.asarray(x).astype(np.float64)


B, N, VD, QD, D, H, NG, P = 32, 36, 2048, 1024, 1024, 8, 20, 64
DH = D // H


def setup_inputs():
    s = mx_kscale(D)
    return {"out_t": bf(np.random.standard_normal((B, N, H, D)) * 0.7 * s),
            "out_w": bf(np.random.standard_normal((H, D, DH)) / np.sqrt(D) / s[None, :, None]),
            "out_b": bf(np.random.standard_normal(D) * 0.3),
            "self_feat": bf(np.random.standard_normal((B, N, D)) * 0.9),
            "vis": bf(np.maximum(np.random.standard_normal((B, N, D)), 0.0))}


def reference(out_t, out_w, out_b, self_feat, vis):
    t = mxq(f64(out_t), 3, "e4m3").reshape(B * N, H, D).swapaxes(0, 1)
    nb = t @ mxq(f64(out_w), 1, "e4m3")
    neighbor = nb.swapaxes(0, 1).reshape(B, N, D) + f64(out_b)
    imp_rel = np.maximum(f64(self_feat) + neighbor, 0.0)
    return f64(vis) + imp_rel

@@ -1,0 +1,328 @@
+from contextlib import ExitStack
+
+import concourse.mybir as mybir
+from concourse.masks import make_identity
+
+BF16 = mybir.dt.bfloat16
+F32 = mybir.dt.float32
+U32 = mybir.dt.uint32
+U8 = mybir.dt.uint8
+FP8X4 = mybir.dt.float8_e4m3fn_x4
+ADD = mybir.AluOpType.add
+MAX = mybir.AluOpType.max
+
+P = 128
+ROWS = 32 * 36
+T = ROWS // P
+H = 8
+K = 1024
+DH = 128
+D = H * DH
+NB = T * H
+
+TP_BUFS = 6
+ACC_BUFS = 2
+G_BUFS = 3
+C_BUFS = 3
+X_BUFS = 6
+
+FLOPS = 2 * ROWS * H * K * DH
+
+
+def tile_implicitrelationencoder_pb_kernel(tc, out_t, out_w, out_b, self_feat, vis, out):
+    nc = tc.nc
+    x_v = out_t.rearrange("b n h k -> (b n) (h k)").rearrange("(p t) f -> p t f", t=T)
+    w_v = out_w.rearrange("h (s q e) c -> q (h s) (e c)", q=P, e=4)
+    s_v = self_feat.rearrange("b n d -> (b n) d").rearrange("(p t) d -> p t d", t=T)
+    v_v = vis.rearrange("b n d -> (b n) d").rearrange("(p t) d -> p t d", t=T)
+    o_v = out.rearrange("b n d -> (b n) d").rearrange("(p t) d -> p t d", t=T)
+
+    units = []
+    for t in range(T):
+        sizes = [2, 2, 2, 2] if t == T - 1 else [4, 4]
+        h0 = 0
+        for nh in sizes:
+            units.append((t, h0, nh))
+            h0 += nh
+    NU = len(units)
+    first_bank = [H * t + h0 for (t, h0, nh) in units]
+    last_bank = [H * t + h0 + nh - 1 for (t, h0, nh) in units]
+    unit_of_bank = {}
+    for i in range(NU):
+        for n in range(first_bank[i], last_bank[i] + 1):
+            unit_of_bank[n] = i
+
+    queues = {"sync": [], "pe": [], "act": [], "dve": []}
+
+    def op(queue, name, needs, emit):
+        queues[queue].append((name, [x for x in needs if x is not None], emit))
+
+    with ExitStack() as ctx:
+        const = ctx.enter_context(tc.tile_pool(name="const", bufs=1))
+        xpool = ctx.enter_context(tc.tile_pool(name="xpool", bufs=X_BUFS))
+        gpool = ctx.enter_context(tc.tile_pool(name="gpool", bufs=G_BUFS))
+        cpool = ctx.enter_context(tc.tile_pool(name="cpool", bufs=C_BUFS))
+        tpp = ctx.enter_context(tc.psum_pool(name="tpp", bufs=TP_BUFS))
+        accp = ctx.enter_context(tc.psum_pool(name="accp", bufs=ACC_BUFS))
+        ctx.enter_context(tc.manual_schedule())
+
+        brow = const.tile([P, D], BF16)
+        ones = const.tile([P, P], BF16)
+        ident = const.tile([P, P], F32)
+        bias_bc = const.tile([P, D], F32)
+        wcodes = const.tile([P, 2 * H * DH], U32, align_bytes=64)
+        wscl = const.tile([P, 2 * H * DH], U8, align_bytes=64)
+        self_sb = [const.tile([P, 3, D], BF16, name="self%d" % i) for i in range(3)]
+        vis_sb = [const.tile([P, 3, D], BF16, name="vis%d" % i) for i in range(3)]
+        res = [const.tile([P, 3, D], F32, name="res%d" % i) for i in range(3)]
+
+        nc.gpsimd.memset(brow[:], 0.0)
+        nc.gpsimd.memset(ones[:], 1.0)
+        make_identity(nc, ident[:])
+
+        xt = {}
+        tps = {}
+        gts = {}
+        cds = {}
+        accs = {}
+
+        def load_w(a):
+            if a == 0:
+                wraw = xpool.tile([P, H * K], BF16, tag="x")
+                xt["w"] = wraw
+            nc.sync.dma_start(
+                out=xt["w"][:, 4096 * a : 4096 * (a + 1)].rearrange("p (b f) -> p b f", f=512),
+                in_=w_v[:, 8 * a : 8 * (a + 1), :],
+            )
+
+        def load_bias():
+            nc.sync.dma_start(out=brow[0:1, :], in_=out_b.rearrange("(o d) -> o d", o=1))
+
+        def load_self(i):
+            nc.sync.dma_start(out=self_sb[i][:], in_=s_v[:, 3 * i : 3 * i + 3, :])
+
+        def load_vis(i):
+            nc.sync.dma_start(out=vis_sb[i][:], in_=v_v[:, 3 * i : 3 * i + 3, :])
+
+        def load_x(i):
+            t, h0, nh = units[i]
+            if h0 == 0:
+                xtile = xpool.tile([P, H * K], BF16, tag="x")
+                xt[t] = xtile
+            nc.sync.dma_start(out=xt[t][:, K * h0 : K * (h0 + nh)], in_=x_v[:, t, K * h0 : K * (h0 + nh)])
+
+        def queue_x(t):
+            if t < X_BUFS - 1:
+                slot = None
+            elif t == X_BUFS - 1:
+                slot = "R15"
+            else:
+                slot = "TB%d" % (H * (t - X_BUFS) + H - 1)
+            for i in range(NU):
+                if units[i][0] == t:
+                    op("sync", "x%d" % i, [slot], lambda i=i: load_x(i))
+
+        op("sync", "w0", [], lambda: load_w(0))
+        op("sync", "bias", [], load_bias)
+        op("sync", "self0", [], lambda: load_self(0))
+        op("sync", "w1", [], lambda: load_w(1))
+        op("sync", "self1", [], lambda: load_self(1))
+        op("sync", "self2", [], lambda: load_self(2))
+        for t in range(T):
+            queue_x(t)
+            if t % 3 == 1:
+                op("sync", "vis%d" % (t // 3), [], lambda i=t // 3: load_vis(i))
+
+        def bias_mm(i):
+            bp = tpp.tile([P, 512], F32, tag="tp")
+            tps["b%d" % i] = bp
+            nc.tensor.matmul(bp[:], lhsT=ones[:], rhs=brow[:, 512 * i : 512 * (i + 1)], start=True, stop=True)
+
+        def tb(n):
+            xw = xt[n // H][:].bitcast(F32)
+            hh = n % H
+            tp = tpp.tile([P, 4, P], F32, tag="tp")
+            tps[n] = tp
+            for v in range(4):
+                w0 = 512 * hh + 256 * (v // 2)
+                nc.tensor.transpose(tp[:, v, :], xw[:, w0 + v % 2 : w0 + 256 : 2], ident[:])
+
+        def mx(i):
+            t, h0, nh = units[i]
+            codes, scl = cds[i]
+            acc = accp.tile([P, 512], F32, tag="acc")
+            accs[i] = acc
+            for j in range(nh):
+                h = h0 + j
+                for gp in range(2):
+                    xs = slice(256 * j + 128 * gp, 256 * j + 128 * (gp + 1))
+                    ws = slice(128 * (2 * h + gp), 128 * (2 * h + gp + 1))
+                    nc.tensor.matmul_mx(
+                        out=acc[:, 128 * j : 128 * (j + 1)],
+                        lhsT=codes[:, xs].bitcast(FP8X4),
+                        lhsT_scale=scl[:, xs],
+                        rhs=wcodes[:, ws].bitcast(FP8X4),
+                        rhs_scale=wscl[:, ws],
+                        start=(gp == 0),
+                        stop=(gp == 1),
+                    )
+
+        for i in range(2):
+            op("pe", "bmm%d" % i, ["bias"], lambda i=i: bias_mm(i))
+        for n in range(NB):
+            if n >= TP_BUFS:
+                slot = "C%d" % (n - TP_BUFS)
+            elif n >= TP_BUFS - 2:
+                slot = "bcp%d" % (n - TP_BUFS + 2)
+            else:
+                slot = None
+            op("pe", "TB%d" % n, ["x%d" % unit_of_bank[n], slot], lambda n=n: tb(n))
+            for i in range(NU):
+                if min(last_bank[i] + TP_BUFS, NB - 1) == n:
+                    op(
+                        "pe",
+                        "MX%d" % i,
+                        ["Q%d" % i, "Qw%d" % (units[i][1] // 4), "E1_%d" % (i - ACC_BUFS) if i >= ACC_BUFS else None],
+                        lambda i=i: mx(i),
+                    )
+
+        def bias_copy(i):
+            nc.scalar.copy(out=bias_bc[:, 512 * i : 512 * (i + 1)], in_=tps["b%d" % i][:])
+
+        def regroup_w(b):
+            if b % 8 == 0:
+                wg = gpool.tile([P, 4096], BF16, tag="g", align_bytes=64)
+                gts["w%d" % (b // 8)] = wg
+            nc.scalar.copy(
+                out=gts["w%d" % (b // 8)][:, 512 * (b % 8) : 512 * (b % 8 + 1)].rearrange(
+                    "p (c i t) -> p c t i", i=4, t=4
+                ),
+                in_=xt["w"][:, 512 * b : 512 * (b + 1)].rearrange("p (t c i) -> p c t i", t=4, i=4),
+            )
+
+        def cp(n):
+            i = unit_of_bank[n]
+            j = n - first_bank[i]
+            if j == 0:
+                g = gpool.tile([P, 4096], BF16, tag="g", align_bytes=64)
+                gts[i] = g
+            gw = gts[i][:].bitcast(F32)
+            nc.scalar.copy(
+                out=gw[:, 512 * j : 512 * (j + 1)].rearrange("p (g r u) -> p g r u", g=2, u=2),
+                in_=tps[n][:].rearrange("p (g u) r -> p g r u", u=2),
+            )
+
+        for i in range(2):
+            op("act", "bcp%d" % i, ["bmm%d" % i], lambda i=i: bias_copy(i))
+        for b in range(16):
+            op("act", "R%d" % b, ["w%d" % (b // 8)], lambda b=b: regroup_w(b))
+        g_users = ["Qw0", "Qw1"] + ["Q%d" % i for i in range(NU)]
+        for n in range(NB):
+            i = unit_of_bank[n]
+            slot = None
+            if n == first_bank[i] and i + 2 >= G_BUFS:
+                slot = g_users[i + 2 - G_BUFS]
+            op("act", "C%d" % n, ["TB%d" % n, slot], lambda n=n: cp(n))
+
+        def e0(t):
+            nc.vector.tensor_tensor(
+                out=res[t // 3][:, t % 3, :], in0=self_sb[t // 3][:, t % 3, :], in1=bias_bc[:], op=ADD
+            )
+
+        def quant_w(a):
+            nc.vector.quantize_mx(
+                out=wcodes[:, 1024 * a : 1024 * (a + 1)].bitcast(FP8X4),
+                scales=wscl[:, 1024 * a : 1024 * (a + 1)],
+                in_=gts["w%d" % a][:],
+            )
+
+        def quant(i):
+            nh = units[i][2]
+            codes = cpool.tile([P, 1024], U32, tag="codes", align_bytes=64)
+            scl = cpool.tile([P, 1024], U8, tag="scl", align_bytes=64)
+            cds[i] = (codes, scl)
+            nc.vector.quantize_mx(
+                out=codes[:, : 256 * nh].bitcast(FP8X4), scales=scl[:, : 256 * nh], in_=gts[i][:, : 1024 * nh]
+            )
+
+        def e1(i):
+            t, h0, nh = units[i]
+            rs = res[t // 3][:, t % 3, DH * h0 : DH * (h0 + nh)]
+            nc.vector.tensor_tensor(out=rs, in0=accs[i][:, : DH * nh], in1=rs, op=ADD)
+
+        def e2(i):
+            t, h0, nh = units[i]
+            cols = slice(DH * h0, DH * (h0 + nh))
+            rs = res[t // 3][:, t % 3, cols]
+            nc.vector.scalar_tensor_tensor(
+                out=rs, in0=rs, scalar=0.0, in1=vis_sb[t // 3][:, t % 3, cols], op0=MAX, op1=ADD
+            )
+
+        def q_e0(t):
+            op("dve", "E0_%d" % t, ["self%d" % (t // 3), "bcp1"], lambda: e0(t))
+
+        def q_qw(a):
+            op("dve", "Qw%d" % a, ["R%d" % (8 * a + 7)], lambda: quant_w(a))
+
+        def q_q(i):
+            op(
+                "dve",
+                "Q%d" % i,
+                ["C%d" % last_bank[i], "MX%d" % (i - C_BUFS) if i >= C_BUFS else None],
+                lambda: quant(i),
+            )
+
+        def q_e1(i):
+            if i >= 0:
+                op("dve", "E1_%d" % i, ["MX%d" % i, "E0_%d" % units[i][0]], lambda: e1(i))
+
+        def q_e2(i):
+            if i >= 0:
+                op("dve", "E2_%d" % i, ["E1_%d" % i, "vis%d" % (units[i][0] // 3)], lambda: e2(i))
+
+        for t in range(3):
+            q_e0(t)
+        q_qw(0)
+        for t in range(3, 6):
+            q_e0(t)
+        q_qw(1)
+        for t in range(6, 9):
+            q_e0(t)
+        for i in range(NU):
+            q_q(i)
+            q_e1(i - 1)
+            q_e2(i - 2)
+        q_e2(NU - 2)
+        q_e1(NU - 1)
+        q_e2(NU - 1)
+
+        def store_tiles(t0, t1):
+            nc.sync.dma_start(out=o_v[:, t0:t1, :], in_=res[t0 // 3][:, t0 % 3 : t0 % 3 + t1 - t0, :])
+
+        def store_unit(i):
+            t, h0, nh = units[i]
+            cols = slice(DH * h0, DH * (h0 + nh))
+            nc.sync.dma_start(out=o_v[:, t, cols], in_=res[t // 3][:, t % 3, cols])
+
+        def last_unit(t):
+            return max(i for i in range(NU) if units[i][0] == t)
+
+        for t0, t1 in ((0, 3), (3, 6), (6, 7), (7, 8)):
+            op("sync", "S%d" % t0, ["E2_%d" % last_unit(t1 - 1)], lambda t0=t0, t1=t1: store_tiles(t0, t1))
+        for i in range(NU):
+            if units[i][0] == T - 1:
+                op("sync", "SU%d" % i, ["E2_%d" % i], lambda i=i: store_unit(i))
+
+        done = set()
+        heads = {"sync": 0, "pe": 0, "act": 0, "dve": 0}
+        moved = True
+        while moved:
+            moved = False
+            for q in ("sync", "pe", "act", "dve"):
+                while heads[q] < len(queues[q]) and all(x in done for x in queues[q][heads[q]][1]):
+                    name, needs, emit = queues[q][heads[q]]
+                    emit()
+                    done.add(name)
+                    heads[q] += 1
+                    moved = True
+        assert all(heads[q] == len(queues[q]) for q in heads)

@@ -23,8 +23,13 @@ NB = T * H
 TP_BUFS = 6
 ACC_BUFS = 2
 G_BUFS = 3
-C_BUFS = 3
+C_BUFS = 4
+W_DVE = 4
+MX_LAG = 6
 X_BUFS = 6
+SELF_AFTER = (1, 3)
+VIS_AFTER = (2, 4, 7)
+E0_STEPS = (2, 3, 4, 7, 8, 9)
 
 FLOPS = 2 * ROWS * H * K * DH
 
@@ -45,6 +50,7 @@ def tile_implicitrelationencoder_pb_kernel(tc, out_t, out_w, out_b, self_feat, v
             units.append((t, h0, nh))
             h0 += nh
     NU = len(units)
+    first_last = min(i for i in range(NU) if units[i][0] == T - 1)
     first_bank = [H * t + h0 for (t, h0, nh) in units]
     last_bank = [H * t + h0 + nh - 1 for (t, h0, nh) in units]
     unit_of_bank = {}
@@ -115,7 +121,7 @@ def tile_implicitrelationencoder_pb_kernel(tc, out_t, out_w, out_b, self_feat, v
             if t < X_BUFS - 1:
                 slot = None
             elif t == X_BUFS - 1:
-                slot = "R15"
+                slot = "Qw1"
             else:
                 slot = "TB%d" % (H * (t - X_BUFS) + H - 1)
             for i in range(NU):
@@ -126,12 +132,14 @@ def tile_implicitrelationencoder_pb_kernel(tc, out_t, out_w, out_b, self_feat, v
         op("sync", "bias", [], load_bias)
         op("sync", "self0", [], lambda: load_self(0))
         op("sync", "w1", [], lambda: load_w(1))
-        op("sync", "self1", [], lambda: load_self(1))
-        op("sync", "self2", [], lambda: load_self(2))
         for t in range(T):
             queue_x(t)
-            if t % 3 == 1:
-                op("sync", "vis%d" % (t // 3), [], lambda i=t // 3: load_vis(i))
+            if t == SELF_AFTER[0]:
+                op("sync", "self1", [], lambda: load_self(1))
+            if t == SELF_AFTER[1]:
+                op("sync", "self2", [], lambda: load_self(2))
+            if t in VIS_AFTER:
+                op("sync", "vis%d" % VIS_AFTER.index(t), [], lambda i=VIS_AFTER.index(t): load_vis(i))
 
         def bias_mm(i):
             bp = tpp.tile([P, 512], F32, tag="tp")
@@ -150,7 +158,12 @@ def tile_implicitrelationencoder_pb_kernel(tc, out_t, out_w, out_b, self_feat, v
         def mx(i):
             t, h0, nh = units[i]
             codes, scl = cds[i]
-            acc = accp.tile([P, 512], F32, tag="acc")
+            if t == T - 1:
+                acc4 = tpp.tile([P, 4, P], F32, tag="tp")
+                acc = acc4[:].rearrange("p j c -> p (j c)")
+            else:
+                acc1 = accp.tile([P, 512], F32, tag="acc")
+                acc = acc1[:]
             accs[i] = acc
             for j in range(nh):
                 h = h0 + j
@@ -178,27 +191,41 @@ def tile_implicitrelationencoder_pb_kernel(tc, out_t, out_w, out_b, self_feat, v
                 slot = None
             op("pe", "TB%d" % n, ["x%d" % unit_of_bank[n], slot], lambda n=n: tb(n))
             for i in range(NU):
-                if min(last_bank[i] + TP_BUFS, NB - 1) == n:
+                last_tile = units[i][0] == T - 1
+                if (NB - 1 if last_tile else last_bank[i] + MX_LAG) == n:
+                    if last_tile:
+                        slot = "C%d" % (NB - TP_BUFS + i - first_last)
+                    else:
+                        slot = "E1_%d" % (i - ACC_BUFS) if i >= ACC_BUFS else None
                     op(
                         "pe",
                         "MX%d" % i,
-                        ["Q%d" % i, "Qw%d" % (units[i][1] // 4), "E1_%d" % (i - ACC_BUFS) if i >= ACC_BUFS else None],
+                        ["Q%d" % i, "Qw%d" % (units[i][1] // 4), slot],
                         lambda i=i: mx(i),
                     )
 
         def bias_copy(i):
             nc.scalar.copy(out=bias_bc[:, 512 * i : 512 * (i + 1)], in_=tps["b%d" % i][:])
 
-        def regroup_w(b):
-            if b % 8 == 0:
-                wg = gpool.tile([P, 4096], BF16, tag="g", align_bytes=64)
-                gts["w%d" % (b // 8)] = wg
-            nc.scalar.copy(
-                out=gts["w%d" % (b // 8)][:, 512 * (b % 8) : 512 * (b % 8 + 1)].rearrange(
-                    "p (c i t) -> p c t i", i=4, t=4
-                ),
-                in_=xt["w"][:, 512 * b : 512 * (b + 1)].rearrange("p (t c i) -> p c t i", t=4, i=4),
+        def w_block(b):
+            dst = gts["w%d" % (b // 8)][:, 512 * (b % 8) : 512 * (b % 8 + 1)]
+            raw = xt["w"][:, 512 * b : 512 * (b + 1)]
+            return (
+                dst.rearrange("p (c i t) -> p c t i", i=4, t=4),
+                raw.rearrange("p (t c i) -> p c t i", t=4, i=4),
             )
+
+        def regroup_w_act(b):
+            dst, raw = w_block(b)
+            nc.scalar.copy(out=dst, in_=raw)
+
+        def regroup_w_dve(b):
+            dst, raw = w_block(b)
+            nc.vector.tensor_copy(out=dst, in_=raw)
+
+        def new_wg(a):
+            wg = gpool.tile([P, 4096], BF16, tag="g", align_bytes=64)
+            gts["w%d" % a] = wg
 
         def cp(n):
             i = unit_of_bank[n]
@@ -214,8 +241,11 @@ def tile_implicitrelationencoder_pb_kernel(tc, out_t, out_w, out_b, self_feat, v
 
         for i in range(2):
             op("act", "bcp%d" % i, ["bmm%d" % i], lambda i=i: bias_copy(i))
+        for a in range(2):
+            op("act", "wg%d" % a, [], lambda a=a: new_wg(a))
         for b in range(16):
-            op("act", "R%d" % b, ["w%d" % (b // 8)], lambda b=b: regroup_w(b))
+            if b % 8 >= W_DVE:
+                op("act", "R%d" % b, ["w%d" % (b // 8)], lambda b=b: regroup_w_act(b))
         g_users = ["Qw0", "Qw1"] + ["Q%d" % i for i in range(NU)]
         for n in range(NB):
             i = unit_of_bank[n]
@@ -262,7 +292,11 @@ def tile_implicitrelationencoder_pb_kernel(tc, out_t, out_w, out_b, self_feat, v
             op("dve", "E0_%d" % t, ["self%d" % (t // 3), "bcp1"], lambda: e0(t))
 
         def q_qw(a):
-            op("dve", "Qw%d" % a, ["R%d" % (8 * a + 7)], lambda: quant_w(a))
+            op("dve", "Qw%d" % a, ["R%d" % b for b in range(8 * a, 8 * a + 8)], lambda: quant_w(a))
+
+        def q_rw(a):
+            for b in range(8 * a, 8 * a + W_DVE):
+                op("dve", "R%d" % b, ["w%d" % a, "wg%d" % a], lambda b=b: regroup_w_dve(b))
 
         def q_q(i):
             op(
@@ -280,19 +314,27 @@ def tile_implicitrelationencoder_pb_kernel(tc, out_t, out_w, out_b, self_feat, v
             if i >= 0:
                 op("dve", "E2_%d" % i, ["E1_%d" % i, "vis%d" % (units[i][0] // 3)], lambda: e2(i))
 
-        for t in range(3):
-            q_e0(t)
+        q_rw(0)
+        q_e0(0)
+        q_e0(1)
         q_qw(0)
-        for t in range(3, 6):
-            q_e0(t)
+        q_rw(1)
+        q_e0(2)
         q_qw(1)
-        for t in range(6, 9):
-            q_e0(t)
+        e0_next = 3
+        e2_next = 0
         for i in range(NU):
             q_q(i)
             q_e1(i - 1)
-            q_e2(i - 2)
-        q_e2(NU - 2)
+            if e0_next < T and i in E0_STEPS:
+                q_e0(e0_next)
+                e0_next += 1
+            elif i >= 5:
+                for j in range(e2_next, min(e2_next + 2, i - 1)):
+                    q_e2(j)
+                    e2_next = j + 1
+        for j in range(e2_next, NU - 1):
+            q_e2(j)
         q_e1(NU - 1)
         q_e2(NU - 1)
 

@@ -28,7 +28,7 @@ W_DVE = 4
 MX_LAG = 6
 X_BUFS = 6
 SELF_AFTER = (1, 3)
-VIS_AFTER = (2, 4, 7)
+VIS_AFTER = (2, 5, 7)
 E0_STEPS = (2, 3, 4, 7, 8, 9)
 
 FLOPS = 2 * ROWS * H * K * DH
@@ -44,7 +44,7 @@ def tile_implicitrelationencoder_pb_kernel(tc, out_t, out_w, out_b, self_feat, v
 
     units = []
     for t in range(T):
-        sizes = [2, 2, 2, 2] if t == T - 1 else [4, 4]
+        sizes = [4, 2, 2] if t == T - 1 else [4, 4]
         h0 = 0
         for nh in sizes:
             units.append((t, h0, nh))
@@ -110,12 +110,13 @@ def tile_implicitrelationencoder_pb_kernel(tc, out_t, out_w, out_b, self_feat, v
         def load_vis(i):
             nc.sync.dma_start(out=vis_sb[i][:], in_=v_v[:, 3 * i : 3 * i + 3, :])
 
-        def load_x(i):
-            t, h0, nh = units[i]
+        x_of_bank = {}
+
+        def load_x(t, h0, h1):
             if h0 == 0:
                 xtile = xpool.tile([P, H * K], BF16, tag="x")
                 xt[t] = xtile
-            nc.sync.dma_start(out=xt[t][:, K * h0 : K * (h0 + nh)], in_=x_v[:, t, K * h0 : K * (h0 + nh)])
+            nc.sync.dma_start(out=xt[t][:, K * h0 : K * h1], in_=x_v[:, t, K * h0 : K * h1])
 
         def queue_x(t):
             if t < X_BUFS - 1:
@@ -124,9 +125,10 @@ def tile_implicitrelationencoder_pb_kernel(tc, out_t, out_w, out_b, self_feat, v
                 slot = "Qw1"
             else:
                 slot = "TB%d" % (H * (t - X_BUFS) + H - 1)
-            for i in range(NU):
-                if units[i][0] == t:
-                    op("sync", "x%d" % i, [slot], lambda i=i: load_x(i))
+            for h0, h1 in ((0, 4), (4, H)):
+                op("sync", "x%d_%d" % (t, h0), [slot], lambda h0=h0, h1=h1: load_x(t, h0, h1))
+                for h in range(h0, h1):
+                    x_of_bank[H * t + h] = "x%d_%d" % (t, h0)
 
         op("sync", "w0", [], lambda: load_w(0))
         op("sync", "bias", [], load_bias)
@@ -189,7 +191,7 @@ def tile_implicitrelationencoder_pb_kernel(tc, out_t, out_w, out_b, self_feat, v
                 slot = "bcp%d" % (n - TP_BUFS + 2)
             else:
                 slot = None
-            op("pe", "TB%d" % n, ["x%d" % unit_of_bank[n], slot], lambda n=n: tb(n))
+            op("pe", "TB%d" % n, [x_of_bank[n], slot], lambda n=n: tb(n))
             for i in range(NU):
                 last_tile = units[i][0] == T - 1
                 if (NB - 1 if last_tile else last_bank[i] + MX_LAG) == n:
@@ -323,7 +325,7 @@ def tile_implicitrelationencoder_pb_kernel(tc, out_t, out_w, out_b, self_feat, v
         q_qw(1)
         e0_next = 3
         e2_next = 0
-        for i in range(NU):
+        for i in range(first_last):
             q_q(i)
             q_e1(i - 1)
             if e0_next < T and i in E0_STEPS:
@@ -333,10 +335,23 @@ def tile_implicitrelationencoder_pb_kernel(tc, out_t, out_w, out_b, self_feat, v
                 for j in range(e2_next, min(e2_next + 2, i - 1)):
                     q_e2(j)
                     e2_next = j + 1
-        for j in range(e2_next, NU - 1):
+        for j in range(e2_next, first_last - 1):
             q_e2(j)
-        q_e1(NU - 1)
-        q_e2(NU - 1)
+            e2_next = j + 1
+        q_q(first_last)
+        q_e1(first_last - 1)
+        for i in range(first_last + 1, NU):
+            q_q(i)
+            if e2_next < first_last:
+                q_e2(e2_next)
+                e2_next += 1
+        for i in range(first_last, NU):
+            q_e1(i)
+            if e2_next < i:
+                q_e2(e2_next)
+                e2_next += 1
+        for j in range(e2_next, NU):
+            q_e2(j)
 
         def store_tiles(t0, t1):
             nc.sync.dma_start(out=o_v[:, t0:t1, :], in_=res[t0 // 3][:, t0 % 3 : t0 % 3 + t1 - t0, :])

from contextlib import ExitStack

import concourse.mybir as mybir
from concourse.masks import make_identity

BF16 = mybir.dt.bfloat16
F32 = mybir.dt.float32
U32 = mybir.dt.uint32
U8 = mybir.dt.uint8
FP8X4 = mybir.dt.float8_e4m3fn_x4
ADD = mybir.AluOpType.add
MAX = mybir.AluOpType.max

P = 128
ROWS = 32 * 36
T = ROWS // P
H = 8
K = 1024
DH = 128
D = H * DH
NB = T * H

TP_BUFS = 6
ACC_BUFS = 2
G_BUFS = 3
C_BUFS = 4
W_DVE = 4
MX_LAG = 6
X_BUFS = 6
SELF_AFTER = (1, 3)
VIS_AFTER = (2, 5, 7)
E0_STEPS = (2, 3, 4, 7, 8, 9)

FLOPS = 2 * ROWS * H * K * DH


def tile_implicitrelationencoder_pb_kernel(tc, out_t, out_w, out_b, self_feat, vis, out):
    nc = tc.nc
    x_v = out_t.rearrange("b n h k -> (b n) (h k)").rearrange("(p t) f -> p t f", t=T)
    w_v = out_w.rearrange("h (s q e) c -> q (h s) (e c)", q=P, e=4)
    s_v = self_feat.rearrange("b n d -> (b n) d").rearrange("(p t) d -> p t d", t=T)
    v_v = vis.rearrange("b n d -> (b n) d").rearrange("(p t) d -> p t d", t=T)
    o_v = out.rearrange("b n d -> (b n) d").rearrange("(p t) d -> p t d", t=T)

    units = []
    for t in range(T):
        sizes = [4, 2, 2] if t == T - 1 else [4, 4]
        h0 = 0
        for nh in sizes:
            units.append((t, h0, nh))
            h0 += nh
    NU = len(units)
    first_last = min(i for i in range(NU) if units[i][0] == T - 1)
    first_bank = [H * t + h0 for (t, h0, nh) in units]
    last_bank = [H * t + h0 + nh - 1 for (t, h0, nh) in units]
    unit_of_bank = {}
    for i in range(NU):
        for n in range(first_bank[i], last_bank[i] + 1):
            unit_of_bank[n] = i

    queues = {"sync": [], "pe": [], "act": [], "dve": []}

    def op(queue, name, needs, emit):
        queues[queue].append((name, [x for x in needs if x is not None], emit))

    with ExitStack() as ctx:
        const = ctx.enter_context(tc.tile_pool(name="const", bufs=1))
        xpool = ctx.enter_context(tc.tile_pool(name="xpool", bufs=X_BUFS))
        gpool = ctx.enter_context(tc.tile_pool(name="gpool", bufs=G_BUFS))
        cpool = ctx.enter_context(tc.tile_pool(name="cpool", bufs=C_BUFS))
        tpp = ctx.enter_context(tc.psum_pool(name="tpp", bufs=TP_BUFS))
        accp = ctx.enter_context(tc.psum_pool(name="accp", bufs=ACC_BUFS))
        ctx.enter_context(tc.manual_schedule())

        brow = const.tile([P, D], BF16)
        ones = const.tile([P, P], BF16)
        ident = const.tile([P, P], F32)
        bias_bc = const.tile([P, D], F32)
        wcodes = const.tile([P, 2 * H * DH], U32, align_bytes=64)
        wscl = const.tile([P, 2 * H * DH], U8, align_bytes=64)
        self_sb = [const.tile([P, 3, D], BF16, name="self%d" % i) for i in range(3)]
        vis_sb = [const.tile([P, 3, D], BF16, name="vis%d" % i) for i in range(3)]
        res = [const.tile([P, 3, D], F32, name="res%d" % i) for i in range(3)]

        nc.gpsimd.memset(brow[:], 0.0)
        nc.gpsimd.memset(ones[:], 1.0)
        make_identity(nc, ident[:])

        xt = {}
        tps = {}
        gts = {}
        cds = {}
        accs = {}

        def load_w(a):
            if a == 0:
                wraw = xpool.tile([P, H * K], BF16, tag="x")
                xt["w"] = wraw
            nc.sync.dma_start(
                out=xt["w"][:, 4096 * a : 4096 * (a + 1)].rearrange("p (b f) -> p b f", f=512),
                in_=w_v[:, 8 * a : 8 * (a + 1), :],
            )

        def load_bias():
            nc.sync.dma_start(out=brow[0:1, :], in_=out_b.rearrange("(o d) -> o d", o=1))

        def load_self(i):
            nc.sync.dma_start(out=self_sb[i][:], in_=s_v[:, 3 * i : 3 * i + 3, :])

        def load_vis(i):
            nc.sync.dma_start(out=vis_sb[i][:], in_=v_v[:, 3 * i : 3 * i + 3, :])

        x_of_bank = {}

        def load_x(t, h0, h1):
            if h0 == 0:
                xtile = xpool.tile([P, H * K], BF16, tag="x")
                xt[t] = xtile
            nc.sync.dma_start(out=xt[t][:, K * h0 : K * h1], in_=x_v[:, t, K * h0 : K * h1])

        def queue_x(t):
            if t < X_BUFS - 1:
                slot = None
            elif t == X_BUFS - 1:
                slot = "Qw1"
            else:
                slot = "TB%d" % (H * (t - X_BUFS) + H - 1)
            for h0, h1 in ((0, 4), (4, H)):
                op("sync", "x%d_%d" % (t, h0), [slot], lambda h0=h0, h1=h1: load_x(t, h0, h1))
                for h in range(h0, h1):
                    x_of_bank[H * t + h] = "x%d_%d" % (t, h0)

        op("sync", "w0", [], lambda: load_w(0))
        op("sync", "bias", [], load_bias)
        op("sync", "self0", [], lambda: load_self(0))
        op("sync", "w1", [], lambda: load_w(1))
        for t in range(T):
            queue_x(t)
            if t == SELF_AFTER[0]:
                op("sync", "self1", [], lambda: load_self(1))
            if t == SELF_AFTER[1]:
                op("sync", "self2", [], lambda: load_self(2))
            if t in VIS_AFTER:
                op("sync", "vis%d" % VIS_AFTER.index(t), [], lambda i=VIS_AFTER.index(t): load_vis(i))

        def bias_mm(i):
            bp = tpp.tile([P, 512], F32, tag="tp")
            tps["b%d" % i] = bp
            nc.tensor.matmul(bp[:], lhsT=ones[:], rhs=brow[:, 512 * i : 512 * (i + 1)], start=True, stop=True)

        def tb(n):
            xw = xt[n // H][:].bitcast(F32)
            hh = n % H
            tp = tpp.tile([P, 4, P], F32, tag="tp")
            tps[n] = tp
            for v in range(4):
                w0 = 512 * hh + 256 * (v // 2)
                nc.tensor.transpose(tp[:, v, :], xw[:, w0 + v % 2 : w0 + 256 : 2], ident[:])

        def mx(i):
            t, h0, nh = units[i]
            codes, scl = cds[i]
            if t == T - 1:
                acc4 = tpp.tile([P, 4, P], F32, tag="tp")
                acc = acc4[:].rearrange("p j c -> p (j c)")
            else:
                acc1 = accp.tile([P, 512], F32, tag="acc")
                acc = acc1[:]
            accs[i] = acc
            for j in range(nh):
                h = h0 + j
                for gp in range(2):
                    xs = slice(256 * j + 128 * gp, 256 * j + 128 * (gp + 1))
                    ws = slice(128 * (2 * h + gp), 128 * (2 * h + gp + 1))
                    nc.tensor.matmul_mx(
                        out=acc[:, 128 * j : 128 * (j + 1)],
                        lhsT=codes[:, xs].bitcast(FP8X4),
                        lhsT_scale=scl[:, xs],
                        rhs=wcodes[:, ws].bitcast(FP8X4),
                        rhs_scale=wscl[:, ws],
                        start=(gp == 0),
                        stop=(gp == 1),
                    )

        for i in range(2):
            op("pe", "bmm%d" % i, ["bias"], lambda i=i: bias_mm(i))
        for n in range(NB):
            if n >= TP_BUFS:
                slot = "C%d" % (n - TP_BUFS)
            elif n >= TP_BUFS - 2:
                slot = "bcp%d" % (n - TP_BUFS + 2)
            else:
                slot = None
            op("pe", "TB%d" % n, [x_of_bank[n], slot], lambda n=n: tb(n))
            for i in range(NU):
                last_tile = units[i][0] == T - 1
                if (NB - 1 if last_tile else last_bank[i] + MX_LAG) == n:
                    if last_tile:
                        slot = "C%d" % (NB - TP_BUFS + i - first_last)
                    else:
                        slot = "E1_%d" % (i - ACC_BUFS) if i >= ACC_BUFS else None
                    op(
                        "pe",
                        "MX%d" % i,
                        ["Q%d" % i, "Qw%d" % (units[i][1] // 4), slot],
                        lambda i=i: mx(i),
                    )

        def bias_copy(i):
            nc.scalar.copy(out=bias_bc[:, 512 * i : 512 * (i + 1)], in_=tps["b%d" % i][:])

        def w_block(b):
            dst = gts["w%d" % (b // 8)][:, 512 * (b % 8) : 512 * (b % 8 + 1)]
            raw = xt["w"][:, 512 * b : 512 * (b + 1)]
            return (
                dst.rearrange("p (c i t) -> p c t i", i=4, t=4),
                raw.rearrange("p (t c i) -> p c t i", t=4, i=4),
            )

        def regroup_w_act(b):
            dst, raw = w_block(b)
            nc.scalar.copy(out=dst, in_=raw)

        def regroup_w_dve(b):
            dst, raw = w_block(b)
            nc.vector.tensor_copy(out=dst, in_=raw)

        def new_wg(a):
            wg = gpool.tile([P, 4096], BF16, tag="g", align_bytes=64)
            gts["w%d" % a] = wg

        def cp(n):
            i = unit_of_bank[n]
            j = n - first_bank[i]
            if j == 0:
                g = gpool.tile([P, 4096], BF16, tag="g", align_bytes=64)
                gts[i] = g
            gw = gts[i][:].bitcast(F32)
            nc.scalar.copy(
                out=gw[:, 512 * j : 512 * (j + 1)].rearrange("p (g r u) -> p g r u", g=2, u=2),
                in_=tps[n][:].rearrange("p (g u) r -> p g r u", u=2),
            )

        for i in range(2):
            op("act", "bcp%d" % i, ["bmm%d" % i], lambda i=i: bias_copy(i))
        for a in range(2):
            op("act", "wg%d" % a, [], lambda a=a: new_wg(a))
        for b in range(16):
            if b % 8 >= W_DVE:
                op("act", "R%d" % b, ["w%d" % (b // 8)], lambda b=b: regroup_w_act(b))
        g_users = ["Qw0", "Qw1"] + ["Q%d" % i for i in range(NU)]
        for n in range(NB):
            i = unit_of_bank[n]
            slot = None
            if n == first_bank[i] and i + 2 >= G_BUFS:
                slot = g_users[i + 2 - G_BUFS]
            op("act", "C%d" % n, ["TB%d" % n, slot], lambda n=n: cp(n))

        def e0(t):
            nc.vector.tensor_tensor(
                out=res[t // 3][:, t % 3, :], in0=self_sb[t // 3][:, t % 3, :], in1=bias_bc[:], op=ADD
            )

        def quant_w(a):
            nc.vector.quantize_mx(
                out=wcodes[:, 1024 * a : 1024 * (a + 1)].bitcast(FP8X4),
                scales=wscl[:, 1024 * a : 1024 * (a + 1)],
                in_=gts["w%d" % a][:],
            )

        def quant(i):
            nh = units[i][2]
            codes = cpool.tile([P, 1024], U32, tag="codes", align_bytes=64)
            scl = cpool.tile([P, 1024], U8, tag="scl", align_bytes=64)
            cds[i] = (codes, scl)
            nc.vector.quantize_mx(
                out=codes[:, : 256 * nh].bitcast(FP8X4), scales=scl[:, : 256 * nh], in_=gts[i][:, : 1024 * nh]
            )

        def e1(i):
            t, h0, nh = units[i]
            rs = res[t // 3][:, t % 3, DH * h0 : DH * (h0 + nh)]
            nc.vector.tensor_tensor(out=rs, in0=accs[i][:, : DH * nh], in1=rs, op=ADD)

        def e2(i):
            t, h0, nh = units[i]
            cols = slice(DH * h0, DH * (h0 + nh))
            rs = res[t // 3][:, t % 3, cols]
            nc.vector.scalar_tensor_tensor(
                out=rs, in0=rs, scalar=0.0, in1=vis_sb[t // 3][:, t % 3, cols], op0=MAX, op1=ADD
            )

        def q_e0(t):
            op("dve", "E0_%d" % t, ["self%d" % (t // 3), "bcp1"], lambda: e0(t))

        def q_qw(a):
            op("dve", "Qw%d" % a, ["R%d" % b for b in range(8 * a, 8 * a + 8)], lambda: quant_w(a))

        def q_rw(a):
            for b in range(8 * a, 8 * a + W_DVE):
                op("dve", "R%d" % b, ["w%d" % a, "wg%d" % a], lambda b=b: regroup_w_dve(b))

        def q_q(i):
            op(
                "dve",
                "Q%d" % i,
                ["C%d" % last_bank[i], "MX%d" % (i - C_BUFS) if i >= C_BUFS else None],
                lambda: quant(i),
            )

        def q_e1(i):
            if i >= 0:
                op("dve", "E1_%d" % i, ["MX%d" % i, "E0_%d" % units[i][0]], lambda: e1(i))

        def q_e2(i):
            if i >= 0:
                op("dve", "E2_%d" % i, ["E1_%d" % i, "vis%d" % (units[i][0] // 3)], lambda: e2(i))

        q_rw(0)
        q_e0(0)
        q_e0(1)
        q_qw(0)
        q_rw(1)
        q_e0(2)
        q_qw(1)
        e0_next = 3
        e2_next = 0
        for i in range(first_last):
            q_q(i)
            q_e1(i - 1)
            if e0_next < T and i in E0_STEPS:
                q_e0(e0_next)
                e0_next += 1
            elif i >= 5:
                for j in range(e2_next, min(e2_next + 2, i - 1)):
                    q_e2(j)
                    e2_next = j + 1
        for j in range(e2_next, first_last - 1):
            q_e2(j)
            e2_next = j + 1
        q_q(first_last)
        q_e1(first_last - 1)
        for i in range(first_last + 1, NU):
            q_q(i)
            if e2_next < first_last:
                q_e2(e2_next)
                e2_next += 1
        for i in range(first_last, NU):
            q_e1(i)
            if e2_next < i:
                q_e2(e2_next)
                e2_next += 1
        for j in range(e2_next, NU):
            q_e2(j)

        def store_tiles(t0, t1):
            nc.sync.dma_start(out=o_v[:, t0:t1, :], in_=res[t0 // 3][:, t0 % 3 : t0 % 3 + t1 - t0, :])

        def store_unit(i):
            t, h0, nh = units[i]
            cols = slice(DH * h0, DH * (h0 + nh))
            nc.sync.dma_start(out=o_v[:, t, cols], in_=res[t // 3][:, t % 3, cols])

        def last_unit(t):
            return max(i for i in range(NU) if units[i][0] == t)

        for t0, t1 in ((0, 3), (3, 6), (6, 7), (7, 8)):
            op("sync", "S%d" % t0, ["E2_%d" % last_unit(t1 - 1)], lambda t0=t0, t1=t1: store_tiles(t0, t1))
        for i in range(NU):
            if units[i][0] == T - 1:
                op("sync", "SU%d" % i, ["E2_%d" % i], lambda i=i: store_unit(i))

        done = set()
        heads = {"sync": 0, "pe": 0, "act": 0, "dve": 0}
        moved = True
        while moved:
            moved = False
            for q in ("sync", "pe", "act", "dve"):
                while heads[q] < len(queues[q]) and all(x in done for x in queues[q][heads[q]][1]):
                    name, needs, emit = queues[q][heads[q]]
                    emit()
                    done.add(name)
                    heads[q] += 1
                    moved = True
        assert all(heads[q] == len(queues[q]) for q in heads)
